import numpy as np
import ml_dtypes


def mxq(x, axis, fmt="e4m3"):
    dtype, down = {"e4m3": (ml_dtypes.float8_e4m3fn, 7), "e5m2": (ml_dtypes.float8_e5m2, 14)}[fmt]
    v = np.moveaxis(np.asarray(x, np.float32).astype(ml_dtypes.bfloat16).astype(np.float64), axis, -1)
    blocks = v.reshape(v.shape[:-1] + (-1, 32))
    amax = np.abs(blocks).max(-1, keepdims=True)
    byte = np.maximum(np.where(amax > 0, np.frexp(amax)[1] - 1 + 127, 0) - down, 1)
    scale = np.exp2(byte - 127.0)
    codes = (blocks / scale).astype(np.float32).astype(dtype).astype(np.float64)
    return np.moveaxis((codes * scale).reshape(v.shape), -1, axis)


WIDE = False


def mx_kscale(k):
    if not WIDE:
        return np.ones(k)
    levels = np.array([10, -10, 5, -5, 0])
    a = np.random.permutation(np.resize(levels, k // 512 * 4)).reshape(k // 512, 4)
    idx = np.arange(k)
    return np.exp2(a[idx // 512, idx % 128 // 32])


BF16 = ml_dtypes.bfloat16


def bf(x):
    return np.asarray(x, np.float32).astype(BF16)


def f64(x):
    return np.asarray(x).astype(np.float64)


B, E, D1, D2, WS1, WS2, H, HID = 8, 512, 32, 32, 8, 8, 16, 2048
NW = (D1 // WS1) * (D2 // WS2)
S = WS1 * WS2
DH = E // H


def setup_inputs():
    n = np.random.standard_normal
    s = mx_kscale(E)
    return {"z_heads": bf(n((B, NW, H, S, DH)) * 0.4 * s.reshape(H, 1, DH)),
            "x": bf(n((B, E, D1, D2))),
            "Wo": bf(n((E, E)) / np.sqrt(E) / s[:, None]),
            "bo": bf(0.1 * n(E))}


def reference(z_heads, x, Wo, bo):
    z = f64(z_heads).transpose(0, 1, 3, 2, 4).reshape(B, NW, S, E)
    z = (mxq(z, 3, "e4m3") @ mxq(f64(Wo), 0, "e4m3")) + f64(bo)
    z = z.reshape(B, D1 // WS1, D2 // WS2, WS1, WS2, E).transpose(0, 1, 3, 2, 4, 5).reshape(B, D1, D2, E)
    z = np.roll(z, (WS1 // 2, WS2 // 2), axis=(1, 2))
    return f64(x).transpose(0, 2, 3, 1) + z

@@ -1,0 +1,191 @@
+from contextlib import ExitStack
+
+import concourse.mybir as mybir
+from concourse.masks import make_identity
+
+BF16 = mybir.dt.bfloat16
+F32 = mybir.dt.float32
+U32 = mybir.dt.uint32
+U8 = mybir.dt.uint8
+FP8X4 = mybir.dt.float8_e4m3fn_x4
+ADD = mybir.AluOpType.add
+MULT = mybir.AluOpType.mult
+
+P = 128
+BATCH = 8
+E = 512
+SIDE = 32
+WIN = 8
+SHIFT = 4
+TOKENS = WIN * WIN
+HALVES = 2 * BATCH
+E_TILES = E // P
+ROWS = 4
+STEPS = 8
+STAGES = 4
+GROUPS = STAGES * E_TILES
+Z_AHEAD = 3
+
+FLOPS = 2 * BATCH * SIDE * SIDE * E * E
+
+
+def tile_functatransformer_pb_t_kernel(tc, z_heads, x, Wo, bo, out):
+    nc = tc.nc
+    with ExitStack() as pools:
+        keep = pools.enter_context(tc.tile_pool(name="keep", bufs=1))
+
+        wo_codes = keep.tile([P, E], U32, align_bytes=64)
+        wo_scales = keep.tile([P, E], U8, align_bytes=64)
+        with tc.tile_pool(name="wo_stage", bufs=1) as wo_stage:
+            wo_rows = wo_stage.tile([P, 4, E], BF16)
+            for u in range(2):
+                nc.sync.dma_start(
+                    out=wo_rows[:, 2 * u : 2 * u + 2, :],
+                    in_=Wo[256 * u : 256 * u + 256, :].rearrange("(q e) c -> q e c", e=2),
+                )
+            wo_grouped = wo_stage.tile([P, E, 4], BF16, align_bytes=64)
+            nc.vector.tensor_copy(out=wo_grouped[:], in_=wo_rows[:].rearrange("p t c -> p c t"))
+            nc.vector.quantize_mx(
+                out=wo_codes[:].bitcast(FP8X4),
+                scales=wo_scales[:],
+                in_=wo_grouped[:].rearrange("p c t -> p (c t)"),
+            )
+
+        sums = pools.enter_context(tc.tile_pool(name="sums", bufs=4, reuse_waits="tile"))
+        z_load = pools.enter_context(tc.tile_pool(name="z_load", bufs=Z_AHEAD))
+        z_sort = pools.enter_context(tc.tile_pool(name="z_sort", bufs=2))
+        z_turn = pools.enter_context(tc.tile_pool(name="z_turn", bufs=2))
+        results = pools.enter_context(tc.tile_pool(name="results", bufs=2))
+        products = pools.enter_context(tc.psum_pool(name="products", bufs=4))
+        turned = pools.enter_context(tc.psum_pool(name="turned", bufs=4))
+
+        identity = keep.tile([P, P], F32)
+        make_identity(nc, identity[:])
+        bias_bf = keep.tile([P, E_TILES], BF16)
+        with nc.allow_non_contiguous_dma(reason="512 bias values, one channel to a partition"):
+            nc.sync.dma_start(out=bias_bf[:], in_=bo.rearrange("(t p) -> p t", p=P))
+        bias = keep.tile([P, E_TILES], F32)
+        nc.vector.tensor_copy(out=bias[:], in_=bias_bf[:])
+
+        x_tiles = {}
+
+        def load_x(et):
+            x_sb = keep.tile([P, BATCH, SIDE * SIDE], BF16, name="x_sb%d" % et)
+            nc.sync.dma_start(
+                out=x_sb[:], in_=x[:, P * et : P * et + P, :, :].rearrange("b e i j -> e b (i j)")
+            )
+            x_tiles[et] = x_sb
+
+        z_codes = keep.tile([P, STEPS, TOKENS * HALVES], U32, align_bytes=64)
+        z_scales = keep.tile([P, STEPS, TOKENS * HALVES], U8, align_bytes=64)
+        z_view = z_heads.rearrange(
+            "b (wh wl wj) (hz a y) s d -> wl wj a (b wh) hz (y s d)", wh=2, wl=2, wj=4, hz=2, a=4, y=2
+        )
+        z_loaded = {}
+
+        def load_z(step):
+            wl, wj = divmod(step, 4)
+            z_in = z_load.tile([P, 2 * TOKENS * 32], BF16)
+            for a in range(4):
+                queue = nc.sync if a < 2 else nc.scalar
+                queue.dma_start(out=z_in[32 * a : 32 * a + 32, :], in_=z_view[wl, wj, a])
+            z_loaded[step] = z_in
+
+        def convert_z(step):
+            z_sorted = z_sort.tile([P, 2 * TOKENS * 32], BF16, align_bytes=64)
+            nc.scalar.copy(
+                out=z_sorted[:].bitcast(F32).rearrange("p (s y w) -> p s y w", y=2, w=16),
+                in_=z_loaded[step][:].bitcast(F32).rearrange("p (y s w) -> p s y w", y=2, w=16),
+            )
+            z_t = z_turn.tile([P, 2 * TOKENS * 32], BF16, align_bytes=64)
+            nc.vector.transpose(out=z_t[:].bitcast(F32), in_=z_sorted[:].bitcast(F32))
+            nc.vector.quantize_mx(
+                out=z_codes[:, step, :].bitcast(FP8X4), scales=z_scales[:, step, :], in_=z_t[:]
+            )
+            if step + Z_AHEAD < STEPS:
+                load_z(step + Z_AHEAD)
+            if step + 1 < E_TILES:
+                load_x(step + 1)
+
+        group_sums = {}
+        half_rows = {}
+
+        def first_row(stage, wh):
+            return (16 * wh + ROWS * stage + SHIFT) % SIDE
+
+        def multiply_add(group):
+            stage, et = divmod(group, E_TILES)
+            wl, half = divmod(stage, 2)
+            sum_t = sums.tile([P, HALVES, ROWS * SIDE], F32)
+            group_sums[group] = sum_t
+            by_half = sum_t[:].rearrange("p (b wh) q -> p b wh q", wh=2)
+            for wh in range(2):
+                q0 = SIDE * first_row(stage, wh)
+                nc.gpsimd.tensor_scalar(
+                    out=by_half[:, :, wh, :],
+                    in0=x_tiles[et][:, :, q0 : q0 + ROWS * SIDE],
+                    scalar1=1.0,
+                    scalar2=bias[:, et : et + 1],
+                    op0=MULT,
+                    op1=ADD,
+                )
+            by_column = sum_t[:].rearrange("p t (r j) -> p t r j", j=SIDE)
+            for wj in range(4):
+                product = products.tile([P, 512], F32)
+                nc.tensor.matmul_mx(
+                    out=product[:],
+                    lhsT=wo_codes[:, P * et : P * et + P].bitcast(FP8X4),
+                    lhsT_scale=wo_scales[:, P * et : P * et + P],
+                    rhs=z_codes[:, 4 * wl + wj, 512 * half : 512 * half + 512].bitcast(FP8X4),
+                    rhs_scale=z_scales[:, 4 * wl + wj, 512 * half : 512 * half + 512],
+                    start=True,
+                    stop=True,
+                )
+                by_token = product[:].rearrange("p (r c t) -> p t r c", r=ROWS, c=WIN)
+                j0 = WIN * wj + SHIFT
+                before_edge = min(WIN, SIDE - j0)
+                pieces = [(0, before_edge, j0)]
+                if before_edge < WIN:
+                    pieces.append((before_edge, WIN - before_edge, 0))
+                for c0, n, j in pieces:
+                    nc.vector.tensor_tensor(
+                        out=by_column[:, :, :, j : j + n],
+                        in0=by_token[:, :, :, c0 : c0 + n],
+                        in1=by_column[:, :, :, j : j + n],
+                        op=ADD,
+                    )
+
+        def flip_store(group):
+            stage, et = divmod(group, E_TILES)
+            side = et % 2
+            for quad in range(HALVES // 4):
+                flipped = turned.tile([P, 4, P], F32)
+                for n in range(4):
+                    nc.tensor.transpose(
+                        flipped[:, n, :], group_sums[group][:, 4 * quad + n, :], identity[:]
+                    )
+                if side == 0:
+                    half_rows[quad] = results.tile([P, 4, 2 * P], F32, name="half_rows%d" % quad)
+                nc.scalar.copy(out=half_rows[quad][:, :, P * side : P * side + P], in_=flipped[:])
+                if side == 1:
+                    e0 = P * (et - 1)
+                    for n in range(4):
+                        b, wh = divmod(4 * quad + n, 2)
+                        i0 = first_row(stage, wh)
+                        nc.sync.dma_start(
+                            out=out[b, i0 : i0 + ROWS, :, e0 : e0 + 2 * P].rearrange("i j e -> (i j) e"),
+                            in_=half_rows[quad][:, n, :],
+                        )
+
+        for step in range(Z_AHEAD):
+            load_z(step)
+        load_x(0)
+        for step in range(STEPS // 2):
+            convert_z(step)
+        for group in range(GROUPS + 1):
+            if group % 2 == 0 and group < STEPS:
+                convert_z(STEPS // 2 + group // 2)
+            if group < GROUPS:
+                multiply_add(group)
+            if group > 0:
+                flip_store(group - 1)

@@ -76,8 +76,8 @@ def tile_functatransformer_pb_t_kernel(tc, z_heads, x, Wo, bo, out):
             )
             x_tiles[et] = x_sb
 
-        z_codes = keep.tile([P, STEPS, TOKENS * HALVES], U32, align_bytes=64)
-        z_scales = keep.tile([P, STEPS, TOKENS * HALVES], U8, align_bytes=64)
+        z_codes = keep.tile([P, 2 * WIN, SIDE * HALVES], U32, align_bytes=64)
+        z_scales = keep.tile([P, 2 * WIN, SIDE * HALVES], U8, align_bytes=64)
         z_view = z_heads.rearrange(
             "b (wh wl wj) (hz a y) s d -> wl wj a (b wh) hz (y s d)", wh=2, wl=2, wj=4, hz=2, a=4, y=2
         )
@@ -99,9 +99,20 @@ def tile_functatransformer_pb_t_kernel(tc, z_heads, x, Wo, bo, out):
             )
             z_t = z_turn.tile([P, 2 * TOKENS * 32], BF16, align_bytes=64)
             nc.vector.transpose(out=z_t[:].bitcast(F32), in_=z_sorted[:].bitcast(F32))
-            nc.vector.quantize_mx(
-                out=z_codes[:, step, :].bitcast(FP8X4), scales=z_scales[:, step, :], in_=z_t[:]
-            )
+            wl, wj = divmod(step, 4)
+            j0 = WIN * wj + SHIFT
+            before_edge = min(WIN, SIDE - j0)
+            pieces = [(0, before_edge, j0)]
+            if before_edge < WIN:
+                pieces.append((before_edge, WIN - before_edge, 0))
+            for si in range(WIN):
+                for c0, n, j in pieces:
+                    token = WIN * si + c0
+                    nc.vector.quantize_mx(
+                        out=z_codes[:, WIN * wl + si, HALVES * j : HALVES * (j + n)].bitcast(FP8X4),
+                        scales=z_scales[:, WIN * wl + si, HALVES * j : HALVES * (j + n)],
+                        in_=z_t[:, 4 * HALVES * token : 4 * HALVES * (token + n)],
+                    )
             if step + Z_AHEAD < STEPS:
                 load_z(step + Z_AHEAD)
             if step + 1 < E_TILES:
@@ -115,7 +126,6 @@ def tile_functatransformer_pb_t_kernel(tc, z_heads, x, Wo, bo, out):
 
         def multiply_add(group):
             stage, et = divmod(group, E_TILES)
-            wl, half = divmod(stage, 2)
             sum_t = sums.tile([P, HALVES, ROWS * SIDE], F32)
             group_sums[group] = sum_t
             by_half = sum_t[:].rearrange("p (b wh) q -> p b wh q", wh=2)
@@ -129,31 +139,24 @@ def tile_functatransformer_pb_t_kernel(tc, z_heads, x, Wo, bo, out):
                     op0=MULT,
                     op1=ADD,
                 )
-            by_column = sum_t[:].rearrange("p t (r j) -> p t r j", j=SIDE)
-            for wj in range(4):
-                product = products.tile([P, 512], F32)
+            by_row = sum_t[:].rearrange("p (b wh) (r j) -> p r b j wh", wh=2, j=SIDE)
+            for r in range(ROWS):
+                product = products.tile([P, SIDE * HALVES], F32)
                 nc.tensor.matmul_mx(
                     out=product[:],
                     lhsT=wo_codes[:, P * et : P * et + P].bitcast(FP8X4),
                     lhsT_scale=wo_scales[:, P * et : P * et + P],
-                    rhs=z_codes[:, 4 * wl + wj, 512 * half : 512 * half + 512].bitcast(FP8X4),
-                    rhs_scale=z_scales[:, 4 * wl + wj, 512 * half : 512 * half + 512],
+                    rhs=z_codes[:, ROWS * stage + r, :].bitcast(FP8X4),
+                    rhs_scale=z_scales[:, ROWS * stage + r, :],
                     start=True,
                     stop=True,
                 )
-                by_token = product[:].rearrange("p (r c t) -> p t r c", r=ROWS, c=WIN)
-                j0 = WIN * wj + SHIFT
-                before_edge = min(WIN, SIDE - j0)
-                pieces = [(0, before_edge, j0)]
-                if before_edge < WIN:
-                    pieces.append((before_edge, WIN - before_edge, 0))
-                for c0, n, j in pieces:
-                    nc.vector.tensor_tensor(
-                        out=by_column[:, :, :, j : j + n],
-                        in0=by_token[:, :, :, c0 : c0 + n],
-                        in1=by_column[:, :, :, j : j + n],
-                        op=ADD,
-                    )
+                nc.vector.tensor_tensor(
+                    out=by_row[:, r],
+                    in0=product[:].rearrange("p (j b wh) -> p b j wh", b=BATCH, wh=2),
+                    in1=by_row[:, r],
+                    op=ADD,
+                )
 
         def flip_store(group):
             stage, et = divmod(group, E_TILES)

@@ -9,7 +9,6 @@ U32 = mybir.dt.uint32
 U8 = mybir.dt.uint8
 FP8X4 = mybir.dt.float8_e4m3fn_x4
 ADD = mybir.AluOpType.add
-MULT = mybir.AluOpType.mult
 
 P = 128
 BATCH = 8
@@ -71,8 +70,13 @@ def tile_functatransformer_pb_t_kernel(tc, z_heads, x, Wo, bo, out):
 
         def load_x(et):
             x_sb = keep.tile([P, BATCH, SIDE * SIDE], BF16, name="x_sb%d" % et)
+            channels = x[:, P * et : P * et + P, :, :]
+            edge = SIDE * (SIDE - SHIFT)
             nc.sync.dma_start(
-                out=x_sb[:], in_=x[:, P * et : P * et + P, :, :].rearrange("b e i j -> e b (i j)")
+                out=x_sb[:, :, :edge], in_=channels[:, :, SHIFT:, :].rearrange("b e i j -> e b (i j)")
+            )
+            nc.sync.dma_start(
+                out=x_sb[:, :, edge:], in_=channels[:, :, :SHIFT, :].rearrange("b e i j -> e b (i j)")
             )
             x_tiles[et] = x_sb
 
@@ -128,18 +132,7 @@ def tile_functatransformer_pb_t_kernel(tc, z_heads, x, Wo, bo, out):
             stage, et = divmod(group, E_TILES)
             sum_t = sums.tile([P, HALVES, ROWS * SIDE], F32)
             group_sums[group] = sum_t
-            by_half = sum_t[:].rearrange("p (b wh) q -> p b wh q", wh=2)
-            for wh in range(2):
-                q0 = SIDE * first_row(stage, wh)
-                nc.gpsimd.tensor_scalar(
-                    out=by_half[:, :, wh, :],
-                    in0=x_tiles[et][:, :, q0 : q0 + ROWS * SIDE],
-                    scalar1=1.0,
-                    scalar2=bias[:, et : et + 1],
-                    op0=MULT,
-                    op1=ADD,
-                )
-            by_row = sum_t[:].rearrange("p (b wh) (r j) -> p r b j wh", wh=2, j=SIDE)
+            x_halves = x_tiles[et][:].rearrange("p b (wh q) -> p (b wh) q", wh=2)
             for r in range(ROWS):
                 product = products.tile([P, SIDE * HALVES], F32)
                 nc.tensor.matmul_mx(
@@ -151,11 +144,14 @@ def tile_functatransformer_pb_t_kernel(tc, z_heads, x, Wo, bo, out):
                     start=True,
                     stop=True,
                 )
-                nc.vector.tensor_tensor(
-                    out=by_row[:, r],
-                    in0=product[:].rearrange("p (j b wh) -> p b j wh", b=BATCH, wh=2),
-                    in1=by_row[:, r],
-                    op=ADD,
+                q0 = SIDE * (ROWS * stage + r)
+                nc.vector.scalar_tensor_tensor(
+                    out=sum_t[:, :, SIDE * r : SIDE * r + SIDE],
+                    in0=product[:].rearrange("p (j t) -> p t j", t=HALVES),
+                    scalar=bias[:, et : et + 1],
+                    in1=x_halves[:, :, q0 : q0 + SIDE],
+                    op0=ADD,
+                    op1=ADD,
                 )
 
         def flip_store(group):

@@ -158,23 +158,24 @@ def tile_functatransformer_pb_t_kernel(tc, z_heads, x, Wo, bo, out):
             stage, et = divmod(group, E_TILES)
             side = et % 2
             for quad in range(HALVES // 4):
+                wh, b0 = quad // 2, 4 * (quad % 2)
                 flipped = turned.tile([P, 4, P], F32)
                 for n in range(4):
                     nc.tensor.transpose(
-                        flipped[:, n, :], group_sums[group][:, 4 * quad + n, :], identity[:]
+                        flipped[:, n, :], group_sums[group][:, 2 * (b0 + n) + wh, :], identity[:]
                     )
                 if side == 0:
                     half_rows[quad] = results.tile([P, 4, 2 * P], F32, name="half_rows%d" % quad)
                 nc.scalar.copy(out=half_rows[quad][:, :, P * side : P * side + P], in_=flipped[:])
                 if side == 1:
                     e0 = P * (et - 1)
-                    for n in range(4):
-                        b, wh = divmod(4 * quad + n, 2)
-                        i0 = first_row(stage, wh)
-                        nc.sync.dma_start(
-                            out=out[b, i0 : i0 + ROWS, :, e0 : e0 + 2 * P].rearrange("i j e -> (i j) e"),
-                            in_=half_rows[quad][:, n, :],
-                        )
+                    i0 = first_row(stage, wh)
+                    nc.gpsimd.dma_start(
+                        out=out[b0 : b0 + 4, i0 : i0 + ROWS, :, e0 : e0 + 2 * P].rearrange(
+                            "b i j e -> (i j) b e"
+                        ),
+                        in_=half_rows[quad][:],
+                    )
 
         for step in range(Z_AHEAD):
             load_z(step)

@@ -15,15 +15,15 @@ BATCH = 8
 E = 512
 SIDE = 32
 WIN = 8
+ACROSS = SIDE // WIN
 SHIFT = 4
-TOKENS = WIN * WIN
-HALVES = 2 * BATCH
-E_TILES = E // P
 ROWS = 4
-STEPS = 8
-STAGES = 4
-GROUPS = STAGES * E_TILES
-Z_AHEAD = 3
+CHUNKS = WIN // ROWS
+CHUNK_TOKENS = ROWS * WIN
+BANK = ACROSS * ROWS * SIDE
+WORDS = E // 4
+E_TILES = E // P
+PAIRS = E_TILES // 2
 
 FLOPS = 2 * BATCH * SIDE * SIDE * E * E
 
@@ -51,12 +51,12 @@ def tile_functatransformer_pb_t_kernel(tc, z_heads, x, Wo, bo, out):
             )
 
         sums = pools.enter_context(tc.tile_pool(name="sums", bufs=4, reuse_waits="tile"))
-        z_load = pools.enter_context(tc.tile_pool(name="z_load", bufs=Z_AHEAD))
+        results = pools.enter_context(tc.tile_pool(name="results", bufs=4))
+        z_load = pools.enter_context(tc.tile_pool(name="z_load", bufs=2))
         z_sort = pools.enter_context(tc.tile_pool(name="z_sort", bufs=2))
-        z_turn = pools.enter_context(tc.tile_pool(name="z_turn", bufs=2))
-        results = pools.enter_context(tc.tile_pool(name="results", bufs=2))
-        products = pools.enter_context(tc.psum_pool(name="products", bufs=4))
-        turned = pools.enter_context(tc.psum_pool(name="turned", bufs=4))
+        z_banks = pools.enter_context(tc.psum_pool(name="z_banks", bufs=2))
+        products = pools.enter_context(tc.psum_pool(name="products", bufs=3))
+        turned = pools.enter_context(tc.psum_pool(name="turned", bufs=3))
 
         identity = keep.tile([P, P], F32)
         make_identity(nc, identity[:])
@@ -80,112 +80,119 @@ def tile_functatransformer_pb_t_kernel(tc, z_heads, x, Wo, bo, out):
             )
             x_tiles[et] = x_sb
 
-        z_codes = keep.tile([P, 2 * WIN, SIDE * HALVES], U32, align_bytes=64)
-        z_scales = keep.tile([P, 2 * WIN, SIDE * HALVES], U8, align_bytes=64)
-        z_view = z_heads.rearrange(
-            "b (wh wl wj) (hz a y) s d -> wl wj a (b wh) hz (y s d)", wh=2, wl=2, wj=4, hz=2, a=4, y=2
-        )
+        z_view = z_heads.rearrange("b w (u h) (c s) d -> u c (b w) h (s d)", u=2, c=CHUNKS)
         z_loaded = {}
+        z_tokens = {}
+        grouped = keep.tile([P, 4 * BATCH * BANK], BF16, align_bytes=64)
+        z_codes = keep.tile([P, CHUNKS, BATCH * BANK], U32, align_bytes=64)
+        z_scales = keep.tile([P, CHUNKS, BATCH * BANK], U8, align_bytes=64)
 
-        def load_z(step):
-            wl, wj = divmod(step, 4)
-            z_in = z_load.tile([P, 2 * TOKENS * 32], BF16)
-            for a in range(4):
-                queue = nc.sync if a < 2 else nc.scalar
-                queue.dma_start(out=z_in[32 * a : 32 * a + 32, :], in_=z_view[wl, wj, a])
-            z_loaded[step] = z_in
+        def load_z(chunk, u):
+            z_in = z_load.tile([P, 8 * CHUNK_TOKENS * 32], BF16)
+            nc.sync.dma_start(out=z_in[:].rearrange("p (h f) -> p h f", h=8), in_=z_view[u, chunk])
+            z_loaded[(chunk, u)] = z_in
 
-        def convert_z(step):
-            z_sorted = z_sort.tile([P, 2 * TOKENS * 32], BF16, align_bytes=64)
-            nc.scalar.copy(
-                out=z_sorted[:].bitcast(F32).rearrange("p (s y w) -> p s y w", y=2, w=16),
-                in_=z_loaded[step][:].bitcast(F32).rearrange("p (y s w) -> p s y w", y=2, w=16),
+        def gather_heads(chunk, u):
+            z_tok = z_sort.tile([P, CHUNK_TOKENS * WORDS], F32)
+            nc.vector.tensor_copy(
+                out=z_tok[:].rearrange("p (s h w) -> p s h w", h=8, w=16),
+                in_=z_loaded[(chunk, u)][:].bitcast(F32).rearrange("p (h s w) -> p s h w", h=8, w=16),
             )
-            z_t = z_turn.tile([P, 2 * TOKENS * 32], BF16, align_bytes=64)
-            nc.vector.transpose(out=z_t[:].bitcast(F32), in_=z_sorted[:].bitcast(F32))
-            wl, wj = divmod(step, 4)
-            j0 = WIN * wj + SHIFT
-            before_edge = min(WIN, SIDE - j0)
-            pieces = [(0, before_edge, j0)]
-            if before_edge < WIN:
-                pieces.append((before_edge, WIN - before_edge, 0))
-            for si in range(WIN):
-                for c0, n, j in pieces:
-                    token = WIN * si + c0
-                    nc.vector.quantize_mx(
-                        out=z_codes[:, WIN * wl + si, HALVES * j : HALVES * (j + n)].bitcast(FP8X4),
-                        scales=z_scales[:, WIN * wl + si, HALVES * j : HALVES * (j + n)],
-                        in_=z_t[:, 4 * HALVES * token : 4 * HALVES * (token + n)],
-                    )
-            if step + Z_AHEAD < STEPS:
-                load_z(step + Z_AHEAD)
-            if step + 1 < E_TILES:
-                load_x(step + 1)
+            z_tokens[(chunk, u)] = z_tok
 
-        group_sums = {}
-        half_rows = {}
-
-        def first_row(stage, wh):
-            return (16 * wh + ROWS * stage + SHIFT) % SIDE
-
-        def multiply_add(group):
-            stage, et = divmod(group, E_TILES)
-            sum_t = sums.tile([P, HALVES, ROWS * SIDE], F32)
-            group_sums[group] = sum_t
-            x_halves = x_tiles[et][:].rearrange("p b (wh q) -> p (b wh) q", wh=2)
-            for r in range(ROWS):
-                product = products.tile([P, SIDE * HALVES], F32)
-                nc.tensor.matmul_mx(
-                    out=product[:],
-                    lhsT=wo_codes[:, P * et : P * et + P].bitcast(FP8X4),
-                    lhsT_scale=wo_scales[:, P * et : P * et + P],
-                    rhs=z_codes[:, ROWS * stage + r, :].bitcast(FP8X4),
-                    rhs_scale=z_scales[:, ROWS * stage + r, :],
-                    start=True,
-                    stop=True,
+        def turn_tokens(chunk, r, m):
+            planes = z_banks.tile([P, 4, P], F32)
+            for q in range(4):
+                token = WIN * r + 2 * m + q // 2
+                nc.tensor.transpose(
+                    planes[:, q, :],
+                    z_tokens[(chunk, q % 2)][:, WORDS * token : WORDS * token + WORDS],
+                    identity[:],
                 )
-                q0 = SIDE * (ROWS * stage + r)
-                nc.vector.scalar_tensor_tensor(
-                    out=sum_t[:, :, SIDE * r : SIDE * r + SIDE],
-                    in0=product[:].rearrange("p (j t) -> p t j", t=HALVES),
-                    scalar=bias[:, et : et + 1],
-                    in1=x_halves[:, :, q0 : q0 + SIDE],
-                    op0=ADD,
-                    op1=ADD,
+            by_window = planes[:].rearrange("p q (v w) -> p v w q", w=ACROSS)
+            by_place = grouped[:].bitcast(F32).rearrange(
+                "p (v r g y) -> p r v g y", r=ROWS, g=ACROSS, y=2 * WIN
+            )
+            carry, column = divmod(2 * m + SHIFT, WIN)
+            pieces = [(0, ACROSS - carry, carry)]
+            if carry > 0:
+                pieces.append((ACROSS - carry, carry, 0))
+            for w0, n, g0 in pieces:
+                nc.scalar.copy(
+                    out=by_place[:, r, :, g0 : g0 + n, 2 * column : 2 * column + 4],
+                    in_=by_window[:, :, w0 : w0 + n, :],
                 )
 
-        def flip_store(group):
-            stage, et = divmod(group, E_TILES)
-            side = et % 2
-            for quad in range(HALVES // 4):
-                wh, b0 = quad // 2, 4 * (quad % 2)
-                flipped = turned.tile([P, 4, P], F32)
-                for n in range(4):
+        def quantise(chunk, b):
+            nc.vector.quantize_mx(
+                out=z_codes[:, chunk, BANK * b : BANK * b + BANK].bitcast(FP8X4),
+                scales=z_scales[:, chunk, BANK * b : BANK * b + BANK],
+                in_=grouped[:, 4 * BANK * b : 4 * BANK * b + 4 * BANK],
+            )
+
+        def multiply_add(chunk, b, et):
+            product = products.tile([P, BANK], F32)
+            nc.tensor.matmul_mx(
+                out=product[:],
+                lhsT=wo_codes[:, P * et : P * et + P].bitcast(FP8X4),
+                lhsT_scale=wo_scales[:, P * et : P * et + P],
+                rhs=z_codes[:, chunk, BANK * b : BANK * b + BANK].bitcast(FP8X4),
+                rhs_scale=z_scales[:, chunk, BANK * b : BANK * b + BANK],
+                start=True,
+                stop=True,
+            )
+            sum_t = sums.tile([P, ACROSS, ROWS * SIDE], F32)
+            nc.vector.scalar_tensor_tensor(
+                out=sum_t[:],
+                in0=product[:].rearrange("p (g q) -> p g q", g=ACROSS),
+                scalar=bias[:, et : et + 1],
+                in1=x_tiles[et][:, b, :].rearrange("p (g c q) -> p c g q", g=ACROSS, c=CHUNKS)[:, chunk],
+                op0=ADD,
+                op1=ADD,
+            )
+            return sum_t
+
+        def flip_store(chunk, pair, b, pair_sums):
+            half_rows = results.tile([P, ACROSS, 2 * P], F32)
+            for side in range(2):
+                flipped = turned.tile([P, ACROSS, P], F32)
+                for g in range(ACROSS):
                     nc.tensor.transpose(
-                        flipped[:, n, :], group_sums[group][:, 2 * (b0 + n) + wh, :], identity[:]
+                        flipped[:, (g + chunk) % ACROSS, :], pair_sums[side][:, g, :], identity[:]
                     )
-                if side == 0:
-                    half_rows[quad] = results.tile([P, 4, 2 * P], F32, name="half_rows%d" % quad)
-                nc.scalar.copy(out=half_rows[quad][:, :, P * side : P * side + P], in_=flipped[:])
-                if side == 1:
-                    e0 = P * (et - 1)
-                    i0 = first_row(stage, wh)
-                    nc.gpsimd.dma_start(
-                        out=out[b0 : b0 + 4, i0 : i0 + ROWS, :, e0 : e0 + 2 * P].rearrange(
-                            "b i j e -> (i j) b e"
-                        ),
-                        in_=half_rows[quad][:],
-                    )
+                nc.scalar.copy(out=half_rows[:, :, P * side : P * side + P], in_=flipped[:])
+            rows = out[b].rearrange("(g c i) j e -> c (i j) g e", g=ACROSS, c=CHUNKS)
+            nc.gpsimd.dma_start(
+                out=rows[1 - chunk][:, :, 2 * P * pair : 2 * P * pair + 2 * P], in_=half_rows[:]
+            )
 
-        for step in range(Z_AHEAD):
-            load_z(step)
+        load_z(0, 0)
+        load_z(0, 1)
         load_x(0)
-        for step in range(STEPS // 2):
-            convert_z(step)
-        for group in range(GROUPS + 1):
-            if group % 2 == 0 and group < STEPS:
-                convert_z(STEPS // 2 + group // 2)
-            if group < GROUPS:
-                multiply_add(group)
-            if group > 0:
-                flip_store(group - 1)
+        load_x(1)
+        gather_heads(0, 0)
+        gather_heads(0, 1)
+        load_z(1, 0)
+        load_z(1, 1)
+        load_x(2)
+        load_x(3)
+        for unit in range(ROWS * 4):
+            turn_tokens(0, unit // 4, unit % 4)
+        gather_heads(1, 0)
+        gather_heads(1, 1)
+
+        waiting = []
+        for chunk in range(CHUNKS):
+            for pair in range(PAIRS):
+                for b in range(BATCH):
+                    if pair == 0:
+                        quantise(chunk, b)
+                    pair_sums = [multiply_add(chunk, b, 2 * pair + side) for side in range(2)]
+                    for args in waiting:
+                        flip_store(*args)
+                    waiting = [(chunk, pair, b, pair_sums)]
+                    if chunk + 1 < CHUNKS and pair == PAIRS - 1:
+                        for unit in (2 * b, 2 * b + 1):
+                            turn_tokens(chunk + 1, unit // 4, unit % 4)
+        for args in waiting:
+            flip_store(*args)

@@ -162,7 +162,7 @@ def tile_functatransformer_pb_t_kernel(tc, z_heads, x, Wo, bo, out):
                     )
                 nc.scalar.copy(out=half_rows[:, :, P * side : P * side + P], in_=flipped[:])
             rows = out[b].rearrange("(g c i) j e -> c (i j) g e", g=ACROSS, c=CHUNKS)
-            nc.gpsimd.dma_start(
+            nc.sync.dma_start(
                 out=rows[1 - chunk][:, :, 2 * P * pair : 2 * P * pair + 2 * P], in_=half_rows[:]
             )
 

@@ -11,188 +11,216 @@ FP8X4 = mybir.dt.float8_e4m3fn_x4
 ADD = mybir.AluOpType.add
 
 P = 128
-BATCH = 8
 E = 512
-SIDE = 32
-WIN = 8
-ACROSS = SIDE // WIN
-SHIFT = 4
-ROWS = 4
-CHUNKS = WIN // ROWS
-CHUNK_TOKENS = ROWS * WIN
-BANK = ACROSS * ROWS * SIDE
-WORDS = E // 4
 E_TILES = E // P
-PAIRS = E_TILES // 2
+GROUPS = 2
+BANDS = 4
+BANK = BANDS * P
+UNITS = 16
+BLOCK = 4
+STEPS = 8
+LEAD = STEPS + 2
 
-FLOPS = 2 * BATCH * SIDE * SIDE * E * E
+FLOPS = 2 * 8 * 32 * 32 * E * E
 
 
 def tile_functatransformer_pb_t_kernel(tc, z_heads, x, Wo, bo, out):
     nc = tc.nc
     with ExitStack() as pools:
         keep = pools.enter_context(tc.tile_pool(name="keep", bufs=1))
+        z_sort = pools.enter_context(tc.tile_pool(name="z_sort", bufs=3))
+        z_group = pools.enter_context(tc.tile_pool(name="z_group", bufs=2))
+        z_mx = pools.enter_context(tc.tile_pool(name="z_mx", bufs=3))
+        z_banks = pools.enter_context(tc.psum_pool(name="z_banks", bufs=2))
+        products = pools.enter_context(tc.psum_pool(name="products", bufs=3))
+        turned = pools.enter_context(tc.psum_pool(name="turned", bufs=3))
+
+        z_view = z_heads.rearrange("(g b) w (u h) s d -> g (b w u) (h s d)", g=GROUPS, u=2)
+
+        identity = keep.tile([P, P], F32)
+        make_identity(nc, identity[:])
+        perms = {}
+        for key in ((0, 0), (0, 1), (1, 0), (1, 1)):
+            perms[key] = keep.tile([P, P], F32, name="perm%d%d" % key)
+        nc.vector.tensor_copy(
+            out=perms[(0, 0)][:].rearrange("p (u w) -> p u w", u=2),
+            in_=identity[:].rearrange("p (w u) -> p u w", u=2),
+        )
+        new = perms[(0, 1)][:].rearrange("p (y a) -> p y a", a=4)
+        old = perms[(0, 0)][:].rearrange("p (y a) -> p y a", a=4)
+        nc.vector.tensor_copy(out=new[:, :, 1:4], in_=old[:, :, 0:3])
+        nc.vector.tensor_copy(out=new[:, :, 0:1], in_=old[:, :, 3:4])
+        for column_turn in range(2):
+            new = perms[(1, column_turn)][:].rearrange("p (y f) -> p y f", f=16)
+            old = perms[(0, column_turn)][:].rearrange("p (y f) -> p y f", f=16)
+            nc.vector.tensor_copy(out=new[:, :, 4:16], in_=old[:, :, 0:12])
+            nc.vector.tensor_copy(out=new[:, :, 0:4], in_=old[:, :, 12:16])
 
         wo_codes = keep.tile([P, E], U32, align_bytes=64)
         wo_scales = keep.tile([P, E], U8, align_bytes=64)
-        with tc.tile_pool(name="wo_stage", bufs=1) as wo_stage:
-            wo_rows = wo_stage.tile([P, 4, E], BF16)
-            for u in range(2):
-                nc.sync.dma_start(
-                    out=wo_rows[:, 2 * u : 2 * u + 2, :],
-                    in_=Wo[256 * u : 256 * u + 256, :].rearrange("(q e) c -> q e c", e=2),
+        bias_bf = keep.tile([P, E_TILES], BF16)
+        bias = keep.tile([P, E_TILES], F32)
+
+        z_raw = {}
+        x_tiles = {}
+
+        def load_z(group):
+            z_in = keep.tile([P, 8 * 64 * 32], BF16, name="z_in%d" % group)
+            nc.sync.dma_start(out=z_in[:], in_=z_view[group])
+            z_raw[group] = z_in
+
+        def load_x(b):
+            x_sb = keep.tile([P, E_TILES, 1024], BF16, name="x_sb%d" % b)
+            nc.sync.dma_start(out=x_sb[:], in_=x[b].rearrange("(t e) i j -> e t (i j)", t=E_TILES))
+            x_tiles[b] = x_sb
+
+        z_tokens = {}
+        z_grouped = {}
+        z_quantised = {}
+
+        def block_place(block):
+            return block // 2, 1 - block % 2
+
+        def gather_heads(step):
+            block, rest = divmod(step, STEPS)
+            group, upper = block_place(block)
+            row, odd = divmod(rest, 2)
+            token = 8 * (4 * (1 - upper) + row) + 4 * (1 - odd)
+            words = z_raw[group][:].bitcast(F32).rearrange("p (h s w) -> p s h w", h=8, w=16)
+            z_tok = z_sort.tile([P, 4 * P], F32)
+            nc.vector.tensor_copy(
+                out=z_tok[:].rearrange("p (s h w) -> p s h w", h=8, w=16),
+                in_=words[:, token : token + 4],
+            )
+            z_tokens[step] = z_tok
+
+        def turn_tokens(step):
+            block, rest = divmod(step, STEPS)
+            group, upper = block_place(block)
+            row, odd = divmod(rest, 2)
+            if rest == 0:
+                grouped = z_group.tile([P, BLOCK * 4 * BANK], BF16, align_bytes=64)
+                z_grouped[block] = grouped
+            planes = z_banks.tile([P, 4 * P], F32)
+            for q in range(4):
+                nc.tensor.transpose(
+                    planes[:, P * q : P * q + P],
+                    z_tokens[step][:, P * q : P * q + P],
+                    perms[(1 - upper, 1 - odd)][:],
                 )
+            nc.scalar.copy(
+                out=z_grouped[block][:]
+                .bitcast(F32)
+                .rearrange("p (v r a o m) -> p r o v a m", r=4, a=4, o=2, m=8)[:, row, odd],
+                in_=planes[:].rearrange("p (m v a) -> p v a m", m=8, a=4),
+            )
+
+        def quantise(unit):
+            block, image = divmod(unit, BLOCK)
+            codes = z_mx.tile([P, BANK], U32, align_bytes=64)
+            scales = z_mx.tile([P, BANK], U8, align_bytes=64)
+            nc.vector.quantize_mx(
+                out=codes[:].bitcast(FP8X4),
+                scales=scales[:],
+                in_=z_grouped[block][:, 4 * BANK * image : 4 * BANK * image + 4 * BANK],
+            )
+            z_quantised[unit] = (codes, scales)
+
+        with tc.tile_pool(name="wo_stage", bufs=1) as wo_stage:
+            load_z(0)
+            wo_rows = wo_stage.tile([P, 4, E], BF16)
+            nc.sync.dma_start(
+                out=wo_rows[:].rearrange("p (u e) c -> p u (e c)", u=2),
+                in_=Wo.rearrange("(u q e) c -> q u (e c)", u=2, e=2),
+            )
+            with nc.allow_non_contiguous_dma(reason="512 bias values, one channel to a partition"):
+                nc.sync.dma_start(out=bias_bf[:], in_=bo.rearrange("(t p) -> p t", p=P))
+            for b in range(4):
+                load_x(b)
+            load_z(1)
+            for b in range(4, 8):
+                load_x(b)
+
+            gather_heads(0)
+            for step in range(STEPS):
+                gather_heads(step + 1)
+                turn_tokens(step)
+
             wo_grouped = wo_stage.tile([P, E, 4], BF16, align_bytes=64)
             nc.vector.tensor_copy(out=wo_grouped[:], in_=wo_rows[:].rearrange("p t c -> p c t"))
+            nc.vector.tensor_copy(out=bias[:], in_=bias_bf[:])
             nc.vector.quantize_mx(
                 out=wo_codes[:].bitcast(FP8X4),
                 scales=wo_scales[:],
                 in_=wo_grouped[:].rearrange("p c t -> p (c t)"),
             )
+            quantise(0)
+            for step in range(STEPS, LEAD):
+                gather_heads(step + 1)
+                turn_tokens(step)
 
-        sums = pools.enter_context(tc.tile_pool(name="sums", bufs=4, reuse_waits="tile"))
-        results = pools.enter_context(tc.tile_pool(name="results", bufs=4))
-        z_load = pools.enter_context(tc.tile_pool(name="z_load", bufs=2))
-        z_sort = pools.enter_context(tc.tile_pool(name="z_sort", bufs=2))
-        z_banks = pools.enter_context(tc.psum_pool(name="z_banks", bufs=2))
-        products = pools.enter_context(tc.psum_pool(name="products", bufs=3))
-        turned = pools.enter_context(tc.psum_pool(name="turned", bufs=3))
+        sums = pools.enter_context(tc.tile_pool(name="sums", bufs=4))
+        results = pools.enter_context(tc.tile_pool(name="results", bufs=6))
 
-        identity = keep.tile([P, P], F32)
-        make_identity(nc, identity[:])
-        bias_bf = keep.tile([P, E_TILES], BF16)
-        with nc.allow_non_contiguous_dma(reason="512 bias values, one channel to a partition"):
-            nc.sync.dma_start(out=bias_bf[:], in_=bo.rearrange("(t p) -> p t", p=P))
-        bias = keep.tile([P, E_TILES], F32)
-        nc.vector.tensor_copy(out=bias[:], in_=bias_bf[:])
-
-        x_tiles = {}
-
-        def load_x(et):
-            x_sb = keep.tile([P, BATCH, SIDE * SIDE], BF16, name="x_sb%d" % et)
-            channels = x[:, P * et : P * et + P, :, :]
-            edge = SIDE * (SIDE - SHIFT)
-            nc.sync.dma_start(
-                out=x_sb[:, :, :edge], in_=channels[:, :, SHIFT:, :].rearrange("b e i j -> e b (i j)")
-            )
-            nc.sync.dma_start(
-                out=x_sb[:, :, edge:], in_=channels[:, :, :SHIFT, :].rearrange("b e i j -> e b (i j)")
-            )
-            x_tiles[et] = x_sb
-
-        z_view = z_heads.rearrange("b w (u h) (c s) d -> u c (b w) h (s d)", u=2, c=CHUNKS)
-        z_loaded = {}
-        z_tokens = {}
-        grouped = keep.tile([P, 4 * BATCH * BANK], BF16, align_bytes=64)
-        z_codes = keep.tile([P, CHUNKS, BATCH * BANK], U32, align_bytes=64)
-        z_scales = keep.tile([P, CHUNKS, BATCH * BANK], U8, align_bytes=64)
-
-        def load_z(chunk, u):
-            z_in = z_load.tile([P, 8 * CHUNK_TOKENS * 32], BF16)
-            nc.sync.dma_start(out=z_in[:].rearrange("p (h f) -> p h f", h=8), in_=z_view[u, chunk])
-            z_loaded[(chunk, u)] = z_in
-
-        def gather_heads(chunk, u):
-            z_tok = z_sort.tile([P, CHUNK_TOKENS * WORDS], F32)
-            nc.vector.tensor_copy(
-                out=z_tok[:].rearrange("p (s h w) -> p s h w", h=8, w=16),
-                in_=z_loaded[(chunk, u)][:].bitcast(F32).rearrange("p (h s w) -> p s h w", h=8, w=16),
-            )
-            z_tokens[(chunk, u)] = z_tok
-
-        def turn_tokens(chunk, r, m):
-            planes = z_banks.tile([P, 4, P], F32)
-            for q in range(4):
-                token = WIN * r + 2 * m + q // 2
-                nc.tensor.transpose(
-                    planes[:, q, :],
-                    z_tokens[(chunk, q % 2)][:, WORDS * token : WORDS * token + WORDS],
-                    identity[:],
-                )
-            by_window = planes[:].rearrange("p q (v w) -> p v w q", w=ACROSS)
-            by_place = grouped[:].bitcast(F32).rearrange(
-                "p (v r g y) -> p r v g y", r=ROWS, g=ACROSS, y=2 * WIN
-            )
-            carry, column = divmod(2 * m + SHIFT, WIN)
-            pieces = [(0, ACROSS - carry, carry)]
-            if carry > 0:
-                pieces.append((ACROSS - carry, carry, 0))
-            for w0, n, g0 in pieces:
-                nc.scalar.copy(
-                    out=by_place[:, r, :, g0 : g0 + n, 2 * column : 2 * column + 4],
-                    in_=by_window[:, :, w0 : w0 + n, :],
-                )
-
-        def quantise(chunk, b):
-            nc.vector.quantize_mx(
-                out=z_codes[:, chunk, BANK * b : BANK * b + BANK].bitcast(FP8X4),
-                scales=z_scales[:, chunk, BANK * b : BANK * b + BANK],
-                in_=grouped[:, 4 * BANK * b : 4 * BANK * b + 4 * BANK],
-            )
-
-        def multiply_add(chunk, b, et):
+        def multiply_add(unit, et):
+            block, image = divmod(unit, BLOCK)
+            group, upper = block_place(block)
+            codes, scales = z_quantised[unit]
             product = products.tile([P, BANK], F32)
             nc.tensor.matmul_mx(
                 out=product[:],
                 lhsT=wo_codes[:, P * et : P * et + P].bitcast(FP8X4),
                 lhsT_scale=wo_scales[:, P * et : P * et + P],
-                rhs=z_codes[:, chunk, BANK * b : BANK * b + BANK].bitcast(FP8X4),
-                rhs_scale=z_scales[:, chunk, BANK * b : BANK * b + BANK],
+                rhs=codes[:].bitcast(FP8X4),
+                rhs_scale=scales[:],
                 start=True,
                 stop=True,
             )
-            sum_t = sums.tile([P, ACROSS, ROWS * SIDE], F32)
+            sum_t = sums.tile([P, BANDS, P], F32)
             nc.vector.scalar_tensor_tensor(
                 out=sum_t[:],
-                in0=product[:].rearrange("p (g q) -> p g q", g=ACROSS),
+                in0=product[:].rearrange("p (g f) -> p g f", g=BANDS),
                 scalar=bias[:, et : et + 1],
-                in1=x_tiles[et][:, b, :].rearrange("p (g c q) -> p c g q", g=ACROSS, c=CHUNKS)[:, chunk],
+                in1=x_tiles[BLOCK * group + image][:, et, :].rearrange(
+                    "p (g h f) -> p h g f", g=BANDS, h=2
+                )[:, upper],
                 op0=ADD,
                 op1=ADD,
             )
             return sum_t
 
-        def flip_store(chunk, pair, b, pair_sums):
-            half_rows = results.tile([P, ACROSS, 2 * P], F32)
-            for side in range(2):
-                flipped = turned.tile([P, ACROSS, P], F32)
-                for g in range(ACROSS):
-                    nc.tensor.transpose(
-                        flipped[:, (g + chunk) % ACROSS, :], pair_sums[side][:, g, :], identity[:]
-                    )
-                nc.scalar.copy(out=half_rows[:, :, P * side : P * side + P], in_=flipped[:])
-            rows = out[b].rearrange("(g c i) j e -> c (i j) g e", g=ACROSS, c=CHUNKS)
-            nc.sync.dma_start(
-                out=rows[1 - chunk][:, :, 2 * P * pair : 2 * P * pair + 2 * P], in_=half_rows[:]
-            )
+        unit_results = {}
 
-        load_z(0, 0)
-        load_z(0, 1)
-        load_x(0)
-        load_x(1)
-        gather_heads(0, 0)
-        gather_heads(0, 1)
-        load_z(1, 0)
-        load_z(1, 1)
-        load_x(2)
-        load_x(3)
-        for unit in range(ROWS * 4):
-            turn_tokens(0, unit // 4, unit % 4)
-        gather_heads(1, 0)
-        gather_heads(1, 1)
+        def flip_store(unit, et, sum_t):
+            block, image = divmod(unit, BLOCK)
+            group, upper = block_place(block)
+            if et == 0:
+                rows = results.tile([P, BANDS, E], F32)
+                unit_results[unit] = rows
+            flipped = turned.tile([P, BANDS, P], F32)
+            for g in range(BANDS):
+                nc.tensor.transpose(flipped[:, g, :], sum_t[:, g, :], identity[:])
+            nc.scalar.copy(out=unit_results[unit][:, :, P * et : P * et + P], in_=flipped[:])
+            if et == E_TILES - 1:
+                nc.sync.dma_start(
+                    out=out[BLOCK * group + image].rearrange(
+                        "(g h i) j e -> h (i j) g e", g=BANDS, h=2
+                    )[upper],
+                    in_=unit_results[unit][:],
+                )
 
         waiting = []
-        for chunk in range(CHUNKS):
-            for pair in range(PAIRS):
-                for b in range(BATCH):
-                    if pair == 0:
-                        quantise(chunk, b)
-                    pair_sums = [multiply_add(chunk, b, 2 * pair + side) for side in range(2)]
-                    for args in waiting:
-                        flip_store(*args)
-                    waiting = [(chunk, pair, b, pair_sums)]
-                    if chunk + 1 < CHUNKS and pair == PAIRS - 1:
-                        for unit in (2 * b, 2 * b + 1):
-                            turn_tokens(chunk + 1, unit // 4, unit % 4)
+        for beat in range(2 * UNITS):
+            unit, half = divmod(beat, 2)
+            pair = [(unit, 2 * half + k, multiply_add(unit, 2 * half + k)) for k in range(2)]
+            for args in waiting:
+                flip_store(*args)
+            waiting = pair
+            if beat + LEAD < STEPS * UNITS // BLOCK:
+                turn_tokens(beat + LEAD)
+            if beat + LEAD + 1 < STEPS * UNITS // BLOCK:
+                gather_heads(beat + LEAD + 1)
+            if half == 0 and unit + 1 < UNITS:
+                quantise(unit + 1)
         for args in waiting:
             flip_store(*args)

@@ -20,6 +20,8 @@ UNITS = 16
 BLOCK = 4
 STEPS = 8
 LEAD = STEPS + 2
+SLOT = 8192
+RESULT_SLOTS = [8, 9, 10, 11, 12, 13, 0, 1, 2, 3, 4, 5, 6, 7, 8, 9]
 
 FLOPS = 2 * 8 * 32 * 32 * E * E
 
@@ -28,6 +30,7 @@ def tile_functatransformer_pb_t_kernel(tc, z_heads, x, Wo, bo, out):
     nc = tc.nc
     with ExitStack() as pools:
         keep = pools.enter_context(tc.tile_pool(name="keep", bufs=1))
+        shared = pools.enter_context(tc.tile_pool(name="shared", bufs=1))
         z_sort = pools.enter_context(tc.tile_pool(name="z_sort", bufs=3))
         z_group = pools.enter_context(tc.tile_pool(name="z_group", bufs=2))
         z_mx = pools.enter_context(tc.tile_pool(name="z_mx", bufs=3))
@@ -65,12 +68,20 @@ def tile_functatransformer_pb_t_kernel(tc, z_heads, x, Wo, bo, out):
         x_tiles = {}
 
         def load_z(group):
-            z_in = keep.tile([P, 8 * 64 * 32], BF16, name="z_in%d" % group)
+            if group == 0:
+                z_in = shared.tile([P, 8 * 64 * 32], BF16, name="z_in0", offset=0)
+            else:
+                z_in = keep.tile([P, 8 * 64 * 32], BF16, name="z_in1")
             nc.sync.dma_start(out=z_in[:], in_=z_view[group])
             z_raw[group] = z_in
 
         def load_x(b):
-            x_sb = keep.tile([P, E_TILES, 1024], BF16, name="x_sb%d" % b)
+            if b < BLOCK:
+                x_sb = shared.tile(
+                    [P, E_TILES, 1024], BF16, name="x_sb%d" % b, offset=SLOT * (BLOCK + b)
+                )
+            else:
+                x_sb = keep.tile([P, E_TILES, 1024], BF16, name="x_sb%d" % b)
             nc.sync.dma_start(out=x_sb[:], in_=x[b].rearrange("(t e) i j -> e t (i j)", t=E_TILES))
             x_tiles[b] = x_sb
 
@@ -160,7 +171,6 @@ def tile_functatransformer_pb_t_kernel(tc, z_heads, x, Wo, bo, out):
                 turn_tokens(step)
 
         sums = pools.enter_context(tc.tile_pool(name="sums", bufs=4))
-        results = pools.enter_context(tc.tile_pool(name="results", bufs=6))
 
         def multiply_add(unit, et):
             block, image = divmod(unit, BLOCK)
@@ -195,7 +205,9 @@ def tile_functatransformer_pb_t_kernel(tc, z_heads, x, Wo, bo, out):
             block, image = divmod(unit, BLOCK)
             group, upper = block_place(block)
             if et == 0:
-                rows = results.tile([P, BANDS, E], F32)
+                rows = shared.tile(
+                    [P, BANDS, E], F32, name="rows%d" % unit, offset=SLOT * RESULT_SLOTS[unit]
+                )
                 unit_results[unit] = rows
             flipped = turned.tile([P, BANDS, P], F32)
             for g in range(BANDS):

@@ -38,26 +38,26 @@ def tile_functatransformer_pb_t_kernel(tc, z_heads, x, Wo, bo, out):
         products = pools.enter_context(tc.psum_pool(name="products", bufs=3))
         turned = pools.enter_context(tc.psum_pool(name="turned", bufs=3))
 
-        z_view = z_heads.rearrange("(g b) w (u h) s d -> g (b w u) (h s d)", g=GROUPS, u=2)
+        z_view = z_heads.rearrange("(g b) w (u h) s d -> g (b w u) h (s d)", g=GROUPS, u=2)
 
         identity = keep.tile([P, P], F32)
         make_identity(nc, identity[:])
         perms = {}
         for key in ((0, 0), (0, 1), (1, 0), (1, 1)):
             perms[key] = keep.tile([P, P], F32, name="perm%d%d" % key)
-        nc.vector.tensor_copy(
+        nc.scalar.copy(
             out=perms[(0, 0)][:].rearrange("p (u w) -> p u w", u=2),
             in_=identity[:].rearrange("p (w u) -> p u w", u=2),
         )
         new = perms[(0, 1)][:].rearrange("p (y a) -> p y a", a=4)
         old = perms[(0, 0)][:].rearrange("p (y a) -> p y a", a=4)
-        nc.vector.tensor_copy(out=new[:, :, 1:4], in_=old[:, :, 0:3])
-        nc.vector.tensor_copy(out=new[:, :, 0:1], in_=old[:, :, 3:4])
+        nc.scalar.copy(out=new[:, :, 1:4], in_=old[:, :, 0:3])
+        nc.scalar.copy(out=new[:, :, 0:1], in_=old[:, :, 3:4])
         for column_turn in range(2):
             new = perms[(1, column_turn)][:].rearrange("p (y f) -> p y f", f=16)
             old = perms[(0, column_turn)][:].rearrange("p (y f) -> p y f", f=16)
-            nc.vector.tensor_copy(out=new[:, :, 4:16], in_=old[:, :, 0:12])
-            nc.vector.tensor_copy(out=new[:, :, 0:4], in_=old[:, :, 12:16])
+            nc.scalar.copy(out=new[:, :, 4:16], in_=old[:, :, 0:12])
+            nc.scalar.copy(out=new[:, :, 0:4], in_=old[:, :, 12:16])
 
         wo_codes = keep.tile([P, E], U32, align_bytes=64)
         wo_scales = keep.tile([P, E], U8, align_bytes=64)
@@ -67,13 +67,16 @@ def tile_functatransformer_pb_t_kernel(tc, z_heads, x, Wo, bo, out):
         z_raw = {}
         x_tiles = {}
 
-        def load_z(group):
-            if group == 0:
-                z_in = shared.tile([P, 8 * 64 * 32], BF16, name="z_in0", offset=0)
-            else:
-                z_in = keep.tile([P, 8 * 64 * 32], BF16, name="z_in1")
-            nc.sync.dma_start(out=z_in[:], in_=z_view[group])
-            z_raw[group] = z_in
+        def load_first_z(lower):
+            z_in = shared.tile([P, 8, 1024], BF16, name="z_in0%d" % lower, offset=2 * SLOT * lower)
+            nc.sync.dma_start(out=z_in[:], in_=z_view[0][:, :, 1024 * lower : 1024 * lower + 1024])
+            z_raw[(0, lower)] = z_in[:]
+
+        def load_second_z():
+            z_in = keep.tile([P, 8, 2048], BF16, name="z_in1")
+            nc.sync.dma_start(out=z_in[:], in_=z_view[1])
+            for lower in range(2):
+                z_raw[(1, lower)] = z_in[:, :, 1024 * lower : 1024 * lower + 1024]
 
         def load_x(b):
             if b < BLOCK:
@@ -96,8 +99,8 @@ def tile_functatransformer_pb_t_kernel(tc, z_heads, x, Wo, bo, out):
             block, rest = divmod(step, STEPS)
             group, upper = block_place(block)
             row, odd = divmod(rest, 2)
-            token = 8 * (4 * (1 - upper) + row) + 4 * (1 - odd)
-            words = z_raw[group][:].bitcast(F32).rearrange("p (h s w) -> p s h w", h=8, w=16)
+            token = 8 * row + 4 * (1 - odd)
+            words = z_raw[(group, 1 - upper)].bitcast(F32).rearrange("p h (s w) -> p s h w", w=16)
             z_tok = z_sort.tile([P, 4 * P], F32)
             nc.vector.tensor_copy(
                 out=z_tok[:].rearrange("p (s h w) -> p s h w", h=8, w=16),
@@ -138,7 +141,7 @@ def tile_functatransformer_pb_t_kernel(tc, z_heads, x, Wo, bo, out):
             z_quantised[unit] = (codes, scales)
 
         with tc.tile_pool(name="wo_stage", bufs=1) as wo_stage:
-            load_z(0)
+            load_first_z(0)
             wo_rows = wo_stage.tile([P, 4, E], BF16)
             nc.sync.dma_start(
                 out=wo_rows[:].rearrange("p (u e) c -> p u (e c)", u=2),
@@ -146,9 +149,11 @@ def tile_functatransformer_pb_t_kernel(tc, z_heads, x, Wo, bo, out):
             )
             with nc.allow_non_contiguous_dma(reason="512 bias values, one channel to a partition"):
                 nc.sync.dma_start(out=bias_bf[:], in_=bo.rearrange("(t p) -> p t", p=P))
-            for b in range(4):
+            load_x(0)
+            load_first_z(1)
+            for b in range(1, 4):
                 load_x(b)
-            load_z(1)
+            load_second_z()
             for b in range(4, 8):
                 load_x(b)
 

@@ -67,16 +67,14 @@ def tile_functatransformer_pb_t_kernel(tc, z_heads, x, Wo, bo, out):
         z_raw = {}
         x_tiles = {}
 
-        def load_first_z(lower):
-            z_in = shared.tile([P, 8, 1024], BF16, name="z_in0%d" % lower, offset=2 * SLOT * lower)
-            nc.sync.dma_start(out=z_in[:], in_=z_view[0][:, :, 1024 * lower : 1024 * lower + 1024])
-            z_raw[(0, lower)] = z_in[:]
-
-        def load_second_z():
-            z_in = keep.tile([P, 8, 2048], BF16, name="z_in1")
-            nc.sync.dma_start(out=z_in[:], in_=z_view[1])
-            for lower in range(2):
-                z_raw[(1, lower)] = z_in[:, :, 1024 * lower : 1024 * lower + 1024]
+        def load_z(group, first, count):
+            if group == 0:
+                z_in = shared.tile([P, 8, 512 * count], BF16, name="z_in0%d" % first, offset=SLOT * first)
+            else:
+                z_in = keep.tile([P, 8, 512 * count], BF16, name="z_in1%d" % first)
+            nc.sync.dma_start(out=z_in[:], in_=z_view[group][:, :, 512 * first : 512 * (first + count)])
+            for k in range(count):
+                z_raw[(group, first + k)] = z_in[:, :, 512 * k : 512 * k + 512]
 
         def load_x(b):
             if b < BLOCK:
@@ -99,8 +97,12 @@ def tile_functatransformer_pb_t_kernel(tc, z_heads, x, Wo, bo, out):
             block, rest = divmod(step, STEPS)
             group, upper = block_place(block)
             row, odd = divmod(rest, 2)
-            token = 8 * row + 4 * (1 - odd)
-            words = z_raw[(group, 1 - upper)].bitcast(F32).rearrange("p h (s w) -> p s h w", w=16)
+            token = 8 * (row % 2) + 4 * (1 - odd)
+            words = (
+                z_raw[(group, 2 * (1 - upper) + row // 2)]
+                .bitcast(F32)
+                .rearrange("p h (s w) -> p s h w", w=16)
+            )
             z_tok = z_sort.tile([P, 4 * P], F32)
             nc.vector.tensor_copy(
                 out=z_tok[:].rearrange("p (s h w) -> p s h w", h=8, w=16),
@@ -141,7 +143,8 @@ def tile_functatransformer_pb_t_kernel(tc, z_heads, x, Wo, bo, out):
             z_quantised[unit] = (codes, scales)
 
         with tc.tile_pool(name="wo_stage", bufs=1) as wo_stage:
-            load_first_z(0)
+            load_z(0, 0, 1)
+            load_z(0, 1, 1)
             wo_rows = wo_stage.tile([P, 4, E], BF16)
             nc.sync.dma_start(
                 out=wo_rows[:].rearrange("p (u e) c -> p u (e c)", u=2),
@@ -150,10 +153,13 @@ def tile_functatransformer_pb_t_kernel(tc, z_heads, x, Wo, bo, out):
             with nc.allow_non_contiguous_dma(reason="512 bias values, one channel to a partition"):
                 nc.sync.dma_start(out=bias_bf[:], in_=bo.rearrange("(t p) -> p t", p=P))
             load_x(0)
-            load_first_z(1)
-            for b in range(1, 4):
-                load_x(b)
-            load_second_z()
+            load_z(0, 2, 1)
+            load_x(1)
+            load_z(0, 3, 1)
+            load_x(2)
+            load_x(3)
+            load_z(1, 0, 2)
+            load_z(1, 2, 2)
             for b in range(4, 8):
                 load_x(b)
 

@@ -29,6 +29,7 @@ FLOPS = 2 * 8 * 32 * 32 * E * E
 def tile_functatransformer_pb_t_kernel(tc, z_heads, x, Wo, bo, out):
     nc = tc.nc
     with ExitStack() as pools:
+        pools.enter_context(tc.manual_schedule(engines={mybir.EngineType.PE}))
         keep = pools.enter_context(tc.tile_pool(name="keep", bufs=1))
         shared = pools.enter_context(tc.tile_pool(name="shared", bufs=1))
         z_sort = pools.enter_context(tc.tile_pool(name="z_sort", bufs=3))
@@ -165,7 +166,8 @@ def tile_functatransformer_pb_t_kernel(tc, z_heads, x, Wo, bo, out):
 
             gather_heads(0)
             for step in range(STEPS):
-                gather_heads(step + 1)
+                if step + 1 < STEPS:
+                    gather_heads(step + 1)
                 turn_tokens(step)
 
             wo_grouped = wo_stage.tile([P, E, 4], BF16, align_bytes=64)
@@ -177,9 +179,8 @@ def tile_functatransformer_pb_t_kernel(tc, z_heads, x, Wo, bo, out):
                 in_=wo_grouped[:].rearrange("p c t -> p (c t)"),
             )
             quantise(0)
-            for step in range(STEPS, LEAD):
-                gather_heads(step + 1)
-                turn_tokens(step)
+            gather_heads(STEPS)
+            gather_heads(STEPS + 1)
 
         sums = pools.enter_context(tc.tile_pool(name="sums", bufs=4))
 
@@ -239,10 +240,17 @@ def tile_functatransformer_pb_t_kernel(tc, z_heads, x, Wo, bo, out):
             for args in waiting:
                 flip_store(*args)
             waiting = pair
-            if beat + LEAD < STEPS * UNITS // BLOCK:
-                turn_tokens(beat + LEAD)
-            if beat + LEAD + 1 < STEPS * UNITS // BLOCK:
-                gather_heads(beat + LEAD + 1)
+            if beat < 2:
+                beat_steps = [STEPS + 2 * beat, STEPS + 2 * beat + 1]
+            else:
+                beat_steps = [beat + LEAD]
+            for step in beat_steps:
+                if step < STEPS * UNITS // BLOCK:
+                    turn_tokens(step)
+            for step in beat_steps:
+                ahead = step + len(beat_steps) if beat != 1 else step + 2 - (step - STEPS - 2)
+                if ahead < STEPS * UNITS // BLOCK and ahead not in z_tokens:
+                    gather_heads(ahead)
             if half == 0 and unit + 1 < UNITS:
                 quantise(unit + 1)
         for args in waiting:

@@ -99,16 +99,22 @@ def tile_functatransformer_pb_t_kernel(tc, z_heads, x, Wo, bo, out):
             group, upper = block_place(block)
             row, odd = divmod(rest, 2)
             token = 8 * (row % 2) + 4 * (1 - odd)
-            words = (
-                z_raw[(group, 2 * (1 - upper) + row // 2)]
-                .bitcast(F32)
-                .rearrange("p h (s w) -> p s h w", w=16)
-            )
-            z_tok = z_sort.tile([P, 4 * P], F32)
-            nc.vector.tensor_copy(
-                out=z_tok[:].rearrange("p (s h w) -> p s h w", h=8, w=16),
-                in_=words[:, token : token + 4],
-            )
+            values = z_raw[(group, 2 * (1 - upper) + row // 2)].rearrange("p h (s d) -> p s h d", d=32)
+            z_tok = z_sort.tile([P, 8 * P], BF16)
+            if block == 0:
+                nc.vector.tensor_copy(
+                    out=z_tok[:].rearrange("p (s h d) -> p s h d", h=8, d=32),
+                    in_=values[:, token : token + 4],
+                )
+            else:
+                nc.gpsimd.tensor_scalar(
+                    out=z_tok[:].rearrange("p (s h d) -> p s h d", h=8, d=32),
+                    in0=values[:, token : token + 4],
+                    scalar1=1.0,
+                    scalar2=0.0,
+                    op0=mybir.AluOpType.mult,
+                    op1=ADD,
+                )
             z_tokens[step] = z_tok
 
         def turn_tokens(step):
@@ -122,7 +128,7 @@ def tile_functatransformer_pb_t_kernel(tc, z_heads, x, Wo, bo, out):
             for q in range(4):
                 nc.tensor.transpose(
                     planes[:, P * q : P * q + P],
-                    z_tokens[step][:, P * q : P * q + P],
+                    z_tokens[step][:].bitcast(F32)[:, P * q : P * q + P],
                     perms[(1 - upper, 1 - odd)][:],
                 )
             nc.scalar.copy(

@@ -32,7 +32,7 @@ def tile_functatransformer_pb_t_kernel(tc, z_heads, x, Wo, bo, out):
         pools.enter_context(tc.manual_schedule(engines={mybir.EngineType.PE}))
         keep = pools.enter_context(tc.tile_pool(name="keep", bufs=1))
         shared = pools.enter_context(tc.tile_pool(name="shared", bufs=1))
-        z_sort = pools.enter_context(tc.tile_pool(name="z_sort", bufs=3))
+        z_sort = pools.enter_context(tc.tile_pool(name="z_sort", bufs=4))
         z_group = pools.enter_context(tc.tile_pool(name="z_group", bufs=2))
         z_mx = pools.enter_context(tc.tile_pool(name="z_mx", bufs=3))
         z_banks = pools.enter_context(tc.psum_pool(name="z_banks", bufs=2))
@@ -185,8 +185,8 @@ def tile_functatransformer_pb_t_kernel(tc, z_heads, x, Wo, bo, out):
                 in_=wo_grouped[:].rearrange("p c t -> p (c t)"),
             )
             quantise(0)
-            gather_heads(STEPS)
-            gather_heads(STEPS + 1)
+            for step in range(STEPS, STEPS + 4):
+                gather_heads(step)
 
         sums = pools.enter_context(tc.tile_pool(name="sums", bufs=4))
 
@@ -253,10 +253,8 @@ def tile_functatransformer_pb_t_kernel(tc, z_heads, x, Wo, bo, out):
             for step in beat_steps:
                 if step < STEPS * UNITS // BLOCK:
                     turn_tokens(step)
-            for step in beat_steps:
-                ahead = step + len(beat_steps) if beat != 1 else step + 2 - (step - STEPS - 2)
-                if ahead < STEPS * UNITS // BLOCK and ahead not in z_tokens:
-                    gather_heads(ahead)
+            if beat + LEAD + 2 < STEPS * UNITS // BLOCK:
+                gather_heads(beat + LEAD + 2)
             if half == 0 and unit + 1 < UNITS:
                 quantise(unit + 1)
         for args in waiting:

@@ -29,7 +29,7 @@ FLOPS = 2 * 8 * 32 * 32 * E * E
 def tile_functatransformer_pb_t_kernel(tc, z_heads, x, Wo, bo, out):
     nc = tc.nc
     with ExitStack() as pools:
-        pools.enter_context(tc.manual_schedule(engines={mybir.EngineType.PE}))
+        pools.enter_context(tc.manual_schedule(engines={mybir.EngineType.PE, mybir.EngineType.DVE}))
         keep = pools.enter_context(tc.tile_pool(name="keep", bufs=1))
         shared = pools.enter_context(tc.tile_pool(name="shared", bufs=1))
         z_sort = pools.enter_context(tc.tile_pool(name="z_sort", bufs=4))

from contextlib import ExitStack

import concourse.mybir as mybir
from concourse.masks import make_identity

BF16 = mybir.dt.bfloat16
F32 = mybir.dt.float32
U32 = mybir.dt.uint32
U8 = mybir.dt.uint8
FP8X4 = mybir.dt.float8_e4m3fn_x4
ADD = mybir.AluOpType.add

P = 128
E = 512
E_TILES = E // P
GROUPS = 2
BANDS = 4
BANK = BANDS * P
UNITS = 16
BLOCK = 4
STEPS = 8
LEAD = STEPS + 2
SLOT = 8192
RESULT_SLOTS = [8, 9, 10, 11, 12, 13, 0, 1, 2, 3, 4, 5, 6, 7, 8, 9]

FLOPS = 2 * 8 * 32 * 32 * E * E


def tile_functatransformer_pb_t_kernel(tc, z_heads, x, Wo, bo, out):
    nc = tc.nc
    with ExitStack() as pools:
        pools.enter_context(tc.manual_schedule(engines={mybir.EngineType.PE, mybir.EngineType.DVE}))
        keep = pools.enter_context(tc.tile_pool(name="keep", bufs=1))
        shared = pools.enter_context(tc.tile_pool(name="shared", bufs=1))
        z_sort = pools.enter_context(tc.tile_pool(name="z_sort", bufs=4))
        z_group = pools.enter_context(tc.tile_pool(name="z_group", bufs=2))
        z_mx = pools.enter_context(tc.tile_pool(name="z_mx", bufs=3))
        z_banks = pools.enter_context(tc.psum_pool(name="z_banks", bufs=2))
        products = pools.enter_context(tc.psum_pool(name="products", bufs=3))
        turned = pools.enter_context(tc.psum_pool(name="turned", bufs=3))

        z_view = z_heads.rearrange("(g b) w (u h) s d -> g (b w u) h (s d)", g=GROUPS, u=2)

        identity = keep.tile([P, P], F32)
        make_identity(nc, identity[:])
        perms = {}
        for key in ((0, 0), (0, 1), (1, 0), (1, 1)):
            perms[key] = keep.tile([P, P], F32, name="perm%d%d" % key)
        nc.scalar.copy(
            out=perms[(0, 0)][:].rearrange("p (u w) -> p u w", u=2),
            in_=identity[:].rearrange("p (w u) -> p u w", u=2),
        )
        new = perms[(0, 1)][:].rearrange("p (y a) -> p y a", a=4)
        old = perms[(0, 0)][:].rearrange("p (y a) -> p y a", a=4)
        nc.scalar.copy(out=new[:, :, 1:4], in_=old[:, :, 0:3])
        nc.scalar.copy(out=new[:, :, 0:1], in_=old[:, :, 3:4])
        for column_turn in range(2):
            new = perms[(1, column_turn)][:].rearrange("p (y f) -> p y f", f=16)
            old = perms[(0, column_turn)][:].rearrange("p (y f) -> p y f", f=16)
            nc.scalar.copy(out=new[:, :, 4:16], in_=old[:, :, 0:12])
            nc.scalar.copy(out=new[:, :, 0:4], in_=old[:, :, 12:16])

        wo_codes = keep.tile([P, E], U32, align_bytes=64)
        wo_scales = keep.tile([P, E], U8, align_bytes=64)
        bias_bf = keep.tile([P, E_TILES], BF16)
        bias = keep.tile([P, E_TILES], F32)

        z_raw = {}
        x_tiles = {}

        def load_z(group, first, count):
            if group == 0:
                z_in = shared.tile([P, 8, 512 * count], BF16, name="z_in0%d" % first, offset=SLOT * first)
            else:
                z_in = keep.tile([P, 8, 512 * count], BF16, name="z_in1%d" % first)
            nc.sync.dma_start(out=z_in[:], in_=z_view[group][:, :, 512 * first : 512 * (first + count)])
            for k in range(count):
                z_raw[(group, first + k)] = z_in[:, :, 512 * k : 512 * k + 512]

        def load_x(b):
            if b < BLOCK:
                x_sb = shared.tile(
                    [P, E_TILES, 1024], BF16, name="x_sb%d" % b, offset=SLOT * (BLOCK + b)
                )
            else:
                x_sb = keep.tile([P, E_TILES, 1024], BF16, name="x_sb%d" % b)
            nc.sync.dma_start(out=x_sb[:], in_=x[b].rearrange("(t e) i j -> e t (i j)", t=E_TILES))
            x_tiles[b] = x_sb

        z_tokens = {}
        z_grouped = {}
        z_quantised = {}

        def block_place(block):
            return block // 2, 1 - block % 2

        def gather_heads(step):
            block, rest = divmod(step, STEPS)
            group, upper = block_place(block)
            row, odd = divmod(rest, 2)
            token = 8 * (row % 2) + 4 * (1 - odd)
            values = z_raw[(group, 2 * (1 - upper) + row // 2)].rearrange("p h (s d) -> p s h d", d=32)
            z_tok = z_sort.tile([P, 8 * P], BF16)
            if block == 0:
                nc.vector.tensor_copy(
                    out=z_tok[:].rearrange("p (s h d) -> p s h d", h=8, d=32),
                    in_=values[:, token : token + 4],
                )
            else:
                nc.gpsimd.tensor_scalar(
                    out=z_tok[:].rearrange("p (s h d) -> p s h d", h=8, d=32),
                    in0=values[:, token : token + 4],
                    scalar1=1.0,
                    scalar2=0.0,
                    op0=mybir.AluOpType.mult,
                    op1=ADD,
                )
            z_tokens[step] = z_tok

        def turn_tokens(step):
            block, rest = divmod(step, STEPS)
            group, upper = block_place(block)
            row, odd = divmod(rest, 2)
            if rest == 0:
                grouped = z_group.tile([P, BLOCK * 4 * BANK], BF16, align_bytes=64)
                z_grouped[block] = grouped
            planes = z_banks.tile([P, 4 * P], F32)
            for q in range(4):
                nc.tensor.transpose(
                    planes[:, P * q : P * q + P],
                    z_tokens[step][:].bitcast(F32)[:, P * q : P * q + P],
                    perms[(1 - upper, 1 - odd)][:],
                )
            nc.scalar.copy(
                out=z_grouped[block][:]
                .bitcast(F32)
                .rearrange("p (v r a o m) -> p r o v a m", r=4, a=4, o=2, m=8)[:, row, odd],
                in_=planes[:].rearrange("p (m v a) -> p v a m", m=8, a=4),
            )

        def quantise(unit):
            block, image = divmod(unit, BLOCK)
            codes = z_mx.tile([P, BANK], U32, align_bytes=64)
            scales = z_mx.tile([P, BANK], U8, align_bytes=64)
            nc.vector.quantize_mx(
                out=codes[:].bitcast(FP8X4),
                scales=scales[:],
                in_=z_grouped[block][:, 4 * BANK * image : 4 * BANK * image + 4 * BANK],
            )
            z_quantised[unit] = (codes, scales)

        with tc.tile_pool(name="wo_stage", bufs=1) as wo_stage:
            load_z(0, 0, 1)
            load_z(0, 1, 1)
            wo_rows = wo_stage.tile([P, 4, E], BF16)
            nc.sync.dma_start(
                out=wo_rows[:].rearrange("p (u e) c -> p u (e c)", u=2),
                in_=Wo.rearrange("(u q e) c -> q u (e c)", u=2, e=2),
            )
            with nc.allow_non_contiguous_dma(reason="512 bias values, one channel to a partition"):
                nc.sync.dma_start(out=bias_bf[:], in_=bo.rearrange("(t p) -> p t", p=P))
            load_x(0)
            load_z(0, 2, 1)
            load_x(1)
            load_z(0, 3, 1)
            load_x(2)
            load_x(3)
            load_z(1, 0, 2)
            load_z(1, 2, 2)
            for b in range(4, 8):
                load_x(b)

            gather_heads(0)
            for step in range(STEPS):
                if step + 1 < STEPS:
                    gather_heads(step + 1)
                turn_tokens(step)

            wo_grouped = wo_stage.tile([P, E, 4], BF16, align_bytes=64)
            nc.vector.tensor_copy(out=wo_grouped[:], in_=wo_rows[:].rearrange("p t c -> p c t"))
            nc.vector.tensor_copy(out=bias[:], in_=bias_bf[:])
            nc.vector.quantize_mx(
                out=wo_codes[:].bitcast(FP8X4),
                scales=wo_scales[:],
                in_=wo_grouped[:].rearrange("p c t -> p (c t)"),
            )
            quantise(0)
            for step in range(STEPS, STEPS + 4):
                gather_heads(step)

        sums = pools.enter_context(tc.tile_pool(name="sums", bufs=4))

        def multiply_add(unit, et):
            block, image = divmod(unit, BLOCK)
            group, upper = block_place(block)
            codes, scales = z_quantised[unit]
            product = products.tile([P, BANK], F32)
            nc.tensor.matmul_mx(
                out=product[:],
                lhsT=wo_codes[:, P * et : P * et + P].bitcast(FP8X4),
                lhsT_scale=wo_scales[:, P * et : P * et + P],
                rhs=codes[:].bitcast(FP8X4),
                rhs_scale=scales[:],
                start=True,
                stop=True,
            )
            sum_t = sums.tile([P, BANDS, P], F32)
            nc.vector.scalar_tensor_tensor(
                out=sum_t[:],
                in0=product[:].rearrange("p (g f) -> p g f", g=BANDS),
                scalar=bias[:, et : et + 1],
                in1=x_tiles[BLOCK * group + image][:, et, :].rearrange(
                    "p (g h f) -> p h g f", g=BANDS, h=2
                )[:, upper],
                op0=ADD,
                op1=ADD,
            )
            return sum_t

        unit_results = {}

        def flip_store(unit, et, sum_t):
            block, image = divmod(unit, BLOCK)
            group, upper = block_place(block)
            if et == 0:
                rows = shared.tile(
                    [P, BANDS, E], F32, name="rows%d" % unit, offset=SLOT * RESULT_SLOTS[unit]
                )
                unit_results[unit] = rows
            flipped = turned.tile([P, BANDS, P], F32)
            for g in range(BANDS):
                nc.tensor.transpose(flipped[:, g, :], sum_t[:, g, :], identity[:])
            nc.scalar.copy(out=unit_results[unit][:, :, P * et : P * et + P], in_=flipped[:])
            if et == E_TILES - 1:
                nc.sync.dma_start(
                    out=out[BLOCK * group + image].rearrange(
                        "(g h i) j e -> h (i j) g e", g=BANDS, h=2
                    )[upper],
                    in_=unit_results[unit][:],
                )

        waiting = []
        for beat in range(2 * UNITS):
            unit, half = divmod(beat, 2)
            pair = [(unit, 2 * half + k, multiply_add(unit, 2 * half + k)) for k in range(2)]
            for args in waiting:
                flip_store(*args)
            waiting = pair
            if beat < 2:
                beat_steps = [STEPS + 2 * beat, STEPS + 2 * beat + 1]
            else:
                beat_steps = [beat + LEAD]
            for step in beat_steps:
                if step < STEPS * UNITS // BLOCK:
                    turn_tokens(step)
            if beat + LEAD + 2 < STEPS * UNITS // BLOCK:
                gather_heads(beat + LEAD + 2)
            if half == 0 and unit + 1 < UNITS:
                quantise(unit + 1)
        for args in waiting:
            flip_store(*args)
